import numpy as np
import ml_dtypes


def mxq(x, axis, fmt="e4m3"):
    dtype, down = {"e4m3": (ml_dtypes.float8_e4m3fn, 7), "e5m2": (ml_dtypes.float8_e5m2, 14)}[fmt]
    v = np.moveaxis(np.asarray(x, np.float32).astype(ml_dtypes.bfloat16).astype(np.float64), axis, -1)
    blocks = v.reshape(v.shape[:-1] + (-1, 32))
    amax = np.abs(blocks).max(-1, keepdims=True)
    byte = np.maximum(np.where(amax > 0, np.frexp(amax)[1] - 1 + 127, 0) - down, 1)
    scale = np.exp2(byte - 127.0)
    codes = (blocks / scale).astype(np.float32).astype(dtype).astype(np.float64)
    return np.moveaxis((codes * scale).reshape(v.shape), -1, axis)


WIDE = False


def mx_kscale(k):
    if not WIDE:
        return np.ones(k)
    levels = np.array([10, -10, 5, -5, 0])
    if k % 512:
        return np.exp2(np.random.permutation(np.resize(levels, k // 32))).repeat(32)
    a = np.empty((k // 512, 16))
    for p in range(k // 512):
        a[p, :8] = np.random.permutation(np.resize(levels, 8))
        for g in range(8):
            far = levels[np.abs(levels - a[p, g]) >= 10]
            a[p, g + 8] = far[np.random.randint(len(far))]
    return np.exp2(a.ravel()).repeat(32)


BF16 = ml_dtypes.bfloat16


def bf(x):
    return np.asarray(x, np.float32).astype(BF16)


def f64(x):
    return np.asarray(x).astype(np.float64)


B, NB, NL, NG, NK = 128, 512, 1536, 500, 3
N2 = 2 * NB


def setup_inputs():
    s = mx_kscale(N2)
    r = s[:NB]
    return {'Volt': bf(np.random.standard_normal((B, N2)) * s),
            'Y_top': bf(np.random.standard_normal((NB, N2)) * 4.0 / np.sqrt(N2) / s[None, :] / r[:, None]),
            'Yconj_top': bf(np.random.standard_normal((NB, N2)) * 4.0 / np.sqrt(N2) / s[None, :] / r[:, None]),
            'PQ_Loads': bf(np.random.standard_normal((B, N2))),
            'PQ_Gens': bf(np.random.standard_normal((B, N2)))}


def reference(Volt, Y_top, Yconj_top, PQ_Loads, PQ_Gens):
    V = f64(Volt)
    Vq = mxq(V, 1, 'e4m3')
    YV = Vq @ mxq(f64(Y_top), 1, 'e4m3').T
    YcV = Vq @ mxq(f64(Yconj_top), 1, 'e4m3').T
    out = np.sum(V[:, :NB] * YV, axis=1) + np.sum(V[:, :NB] * YcV, axis=1)
    pq = f64(PQ_Loads) - f64(PQ_Gens)
    return out + np.sum(pq[:, :NB], axis=1) + np.sum(pq[:, NB:], axis=1)

@@ -1,0 +1,155 @@
+from contextlib import ExitStack
+
+import concourse.mybir as mybir
+from concourse.masks import make_identity
+
+F32 = mybir.dt.float32
+BF16 = mybir.dt.bfloat16
+U32 = mybir.dt.uint32
+U8 = mybir.dt.uint8
+FP8X4 = mybir.dt.float8_e4m3fn_x4
+MULT = mybir.AluOpType.mult
+ADD = mybir.AluOpType.add
+
+P = 128
+K = 1024
+NB = 512
+K_PASS = 512
+PASSES = K // K_PASS
+ROUNDS = NB // P
+BLOCKS = 1 + 2 * ROUNDS
+EARLY = ROUNDS - 1
+HALF = K // 2
+QUAD = 32
+
+FLOPS = 2 * 2 * P * NB * K
+
+
+def tile_kktloss_pc_s_kernel(tc, Volt, Y_top, Yconj_top, PQ_Loads, PQ_Gens, out):
+    nc = tc.nc
+    with ExitStack() as ctx:
+        consts = ctx.enter_context(tc.tile_pool(name="consts", bufs=1))
+        loads = ctx.enter_context(tc.tile_pool(name="loads", bufs=1))
+        stage = ctx.enter_context(tc.tile_pool(name="stage", bufs=4))
+        keep = ctx.enter_context(tc.tile_pool(name="keep", bufs=1))
+        small = ctx.enter_context(tc.tile_pool(name="small", bufs=1))
+        flip_psum = ctx.enter_context(tc.psum_pool(name="flip_psum", bufs=5))
+        acc_psum = ctx.enter_context(tc.psum_pool(name="acc_psum", bufs=1))
+        ctx.enter_context(tc.manual_schedule())
+
+        ident = consts.tile([P, P], F32)
+        make_identity(nc, ident[:])
+
+        sources = [Volt[:, :]]
+        for t in range(ROUNDS):
+            sources.append(Y_top[t * P : (t + 1) * P, :])
+            sources.append(Yconj_top[t * P : (t + 1) * P, :])
+        rows_sb = []
+        for j in range(BLOCKS):
+            block = loads.tile([P, K], BF16, name="rows%d" % j)
+            nc.sync.dma_start(out=block[:], in_=sources[j])
+            rows_sb.append(block)
+        volt_sb = rows_sb[0]
+        loads_sb = loads.tile([P, K], BF16)
+        gens_sb = loads.tile([P, K], BF16)
+        for h in range(2):
+            half = slice(h * HALF, (h + 1) * HALF)
+            nc.sync.dma_start(out=loads_sb[:, half], in_=PQ_Loads[:, half])
+            nc.sync.dma_start(out=gens_sb[:, half], in_=PQ_Gens[:, half])
+
+        codes = keep.tile([P, BLOCKS, PASSES * P], U32, align_bytes=64)
+        scales = keep.tile([P, BLOCKS, PASSES * P], U8, align_bytes=64)
+        parts = small.tile([P, 16], F32)
+        nc.vector.memset(parts[:], 0.0)
+        column = small.tile([P, QUAD], F32, align_bytes=64)
+        nc.vector.memset(column[:], 0.0)
+        grouped = {}
+
+        def flip(j):
+            words = rows_sb[j][:].bitcast(F32)
+            flipped = flip_psum.tile([P, 2 * PASSES, P], F32)
+            for g in range(PASSES):
+                for u in range(2):
+                    every_2nd = words[:, 2 * P * g + u : 2 * P * (g + 1) : 2]
+                    nc.tensor.transpose(flipped[:, 2 * g + u, :], every_2nd, ident[:])
+            grouped[j] = stage.tile([P, K], BF16, align_bytes=64, name="grouped")
+            nc.scalar.copy(
+                out=grouped[j][:].bitcast(F32).rearrange("p (g r u) -> p g r u", g=PASSES, u=2),
+                in_=flipped[:].rearrange("p (g u) r -> p g r u", u=2),
+            )
+
+        def quantise(j):
+            nc.vector.quantize_mx(
+                out=codes[:, j, :].bitcast(FP8X4), scales=scales[:, j, :], in_=grouped[j][:]
+            )
+
+        def multiply(t, acc):
+            for which in range(2):
+                j = 1 + 2 * t + which
+                for g in range(PASSES):
+                    cols = slice(g * P, (g + 1) * P)
+                    nc.tensor.matmul_mx(
+                        out=acc,
+                        lhsT=codes[:, 0, cols].bitcast(FP8X4),
+                        lhsT_scale=scales[:, 0, cols],
+                        rhs=codes[:, j, cols].bitcast(FP8X4),
+                        rhs_scale=scales[:, j, cols],
+                        start=(which == 0 and g == 0),
+                        stop=(which == 1 and g == PASSES - 1),
+                    )
+
+        def weigh(acc, first, width, part):
+            weighted = small.tile([P, width], F32, name="weighted%d" % part)
+            nc.vector.scalar_tensor_tensor(
+                out=weighted[:],
+                in0=acc,
+                scalar=1.0,
+                in1=volt_sb[:, first : first + width],
+                op0=MULT,
+                op1=MULT,
+                accum_out=parts[:, part : part + 1],
+            )
+
+        def balance_on_vector(part):
+            difference = small.tile([P, HALF], F32)
+            nc.vector.scalar_tensor_tensor(
+                out=difference[:],
+                in0=gens_sb[:, 0:HALF],
+                scalar=-1.0,
+                in1=loads_sb[:, 0:HALF],
+                op0=MULT,
+                op1=ADD,
+                accum_out=parts[:, part : part + 1],
+            )
+
+        def balance_on_scalar(part):
+            for n, (source, sign) in enumerate(((loads_sb, 1.0), (gens_sb, -1.0))):
+                signed = small.tile([P, HALF], F32, name="signed%d" % n)
+                nc.scalar.activation(
+                    out=signed[:],
+                    in_=source[:, HALF:K],
+                    func=mybir.ActivationFunctionType.Copy,
+                    scale=sign,
+                    accum_out=parts[:, part + n : part + n + 1],
+                )
+
+        for j in range(BLOCKS - 1):
+            flip(j)
+            quantise(j)
+        flip(BLOCKS - 1)
+        balance_on_vector(2)
+        quantise(BLOCKS - 1)
+        balance_on_scalar(8)
+
+        acc_early = acc_psum.tile([P, EARLY * P], F32)
+        for t in range(EARLY):
+            multiply(t, acc_early[:, t * P : (t + 1) * P])
+        acc_last = acc_psum.tile([P, P], F32)
+        multiply(EARLY, acc_last[:])
+        weigh(acc_early[:], 0, EARLY * P, 0)
+        weigh(acc_last[:], EARLY * P, P, 1)
+
+        nc.vector.tensor_reduce(out=column[:, 0:1], in_=parts[:], axis=mybir.AxisListType.X, op=ADD)
+        turned = small.tile([P, QUAD], F32, align_bytes=64)
+        nc.vector.transpose(out=turned[:], in_=column[:])
+        nc.sync.dma_start(out=out.rearrange("(q r) -> q r", r=QUAD), in_=turned[0:P:QUAD, :])

@@ -18,8 +18,11 @@ K_PASS = 512
 PASSES = K // K_PASS
 ROUNDS = NB // P
 BLOCKS = 1 + 2 * ROUNDS
+LAST = BLOCKS - 1
 EARLY = ROUNDS - 1
 HALF = K // 2
+PARTS = 4
+ON_VECTOR = (3,)
 QUAD = 32
 
 FLOPS = 2 * 2 * P * NB * K
@@ -33,12 +36,14 @@ def tile_kktloss_pc_s_kernel(tc, Volt, Y_top, Yconj_top, PQ_Loads, PQ_Gens, out)
         stage = ctx.enter_context(tc.tile_pool(name="stage", bufs=4))
         keep = ctx.enter_context(tc.tile_pool(name="keep", bufs=1))
         small = ctx.enter_context(tc.tile_pool(name="small", bufs=1))
-        flip_psum = ctx.enter_context(tc.psum_pool(name="flip_psum", bufs=5))
+        flip_psum = ctx.enter_context(tc.psum_pool(name="flip_psum", bufs=6))
         acc_psum = ctx.enter_context(tc.psum_pool(name="acc_psum", bufs=1))
         ctx.enter_context(tc.manual_schedule())
 
         ident = consts.tile([P, P], F32)
         make_identity(nc, ident[:])
+        ones = consts.tile([P, PARTS], F32)
+        nc.gpsimd.memset(ones[:], 1.0)
 
         sources = [Volt[:, :]]
         for t in range(ROUNDS):
@@ -46,41 +51,55 @@ def tile_kktloss_pc_s_kernel(tc, Volt, Y_top, Yconj_top, PQ_Loads, PQ_Gens, out)
             sources.append(Yconj_top[t * P : (t + 1) * P, :])
         rows_sb = []
         for j in range(BLOCKS):
-            block = loads.tile([P, K], BF16, name="rows%d" % j)
-            nc.sync.dma_start(out=block[:], in_=sources[j])
-            rows_sb.append(block)
-        volt_sb = rows_sb[0]
+            pieces = PASSES if j == LAST else 1
+            width = K // pieces
+            tiles = []
+            for n in range(pieces):
+                piece = loads.tile([P, width], BF16, name="rows%d_%d" % (j, n))
+                nc.sync.dma_start(out=piece[:], in_=sources[j][:, n * width : (n + 1) * width])
+                tiles.append(piece)
+            rows_sb.append(tiles)
+        volt_sb = rows_sb[0][0]
         loads_sb = loads.tile([P, K], BF16)
         gens_sb = loads.tile([P, K], BF16)
-        for h in range(2):
-            half = slice(h * HALF, (h + 1) * HALF)
-            nc.sync.dma_start(out=loads_sb[:, half], in_=PQ_Loads[:, half])
-            nc.sync.dma_start(out=gens_sb[:, half], in_=PQ_Gens[:, half])
+        nc.sync.dma_start(out=loads_sb[:], in_=PQ_Loads[:, :])
+        nc.sync.dma_start(out=gens_sb[:], in_=PQ_Gens[:, :])
 
         codes = keep.tile([P, BLOCKS, PASSES * P], U32, align_bytes=64)
         scales = keep.tile([P, BLOCKS, PASSES * P], U8, align_bytes=64)
-        parts = small.tile([P, 16], F32)
-        nc.vector.memset(parts[:], 0.0)
         column = small.tile([P, QUAD], F32, align_bytes=64)
         nc.vector.memset(column[:], 0.0)
-        grouped = {}
 
-        def flip(j):
-            words = rows_sb[j][:].bitcast(F32)
-            flipped = flip_psum.tile([P, 2 * PASSES, P], F32)
-            for g in range(PASSES):
+        acc_last = acc_psum.tile([P, P + PARTS], F32)
+        nc.tensor.matmul(acc_last[:, P:], lhsT=ident[:], rhs=ones[:], start=True, stop=True)
+        weights = small.tile([P, P + PARTS], F32)
+        nc.gpsimd.tensor_copy(out=weights[:, 0:P], in_=volt_sb[:, EARLY * P : NB])
+        parts = weights[:, P : P + PARTS]
+
+        def flip(piece):
+            words = piece[:].bitcast(F32)
+            flipped = flip_psum.tile([P, 2 * PASSES, P], F32, name="flipped")
+            for g in range(piece.shape[1] // K_PASS):
                 for u in range(2):
                     every_2nd = words[:, 2 * P * g + u : 2 * P * (g + 1) : 2]
                     nc.tensor.transpose(flipped[:, 2 * g + u, :], every_2nd, ident[:])
-            grouped[j] = stage.tile([P, K], BF16, align_bytes=64, name="grouped")
-            nc.scalar.copy(
-                out=grouped[j][:].bitcast(F32).rearrange("p (g r u) -> p g r u", g=PASSES, u=2),
-                in_=flipped[:].rearrange("p (g u) r -> p g r u", u=2),
-            )
+            return flipped
 
-        def quantise(j):
+        def copy_out(flipped, passes, copy):
+            grouped = stage.tile([P, K], BF16, align_bytes=64, name="grouped")
+            words = grouped[:].bitcast(F32).rearrange("p (g r u) -> p g r u", g=PASSES, u=2)
+            copy(
+                out=words[:, 0:passes],
+                in_=flipped[:, 0 : 2 * passes].rearrange("p (g u) r -> p g r u", u=2),
+            )
+            return grouped
+
+        def quantise(j, first, passes, grouped):
+            cols = slice(first * P, (first + passes) * P)
             nc.vector.quantize_mx(
-                out=codes[:, j, :].bitcast(FP8X4), scales=scales[:, j, :], in_=grouped[j][:]
+                out=codes[:, j, cols].bitcast(FP8X4),
+                scales=scales[:, j, cols],
+                in_=grouped[:, 0 : passes * K_PASS],
             )
 
         def multiply(t, acc):
@@ -98,58 +117,69 @@ def tile_kktloss_pc_s_kernel(tc, Volt, Y_top, Yconj_top, PQ_Loads, PQ_Gens, out)
                         stop=(which == 1 and g == PASSES - 1),
                     )
 
-        def weigh(acc, first, width, part):
-            weighted = small.tile([P, width], F32, name="weighted%d" % part)
+        def weigh(acc, weight, total, name):
+            weighted = small.tile([P, acc.shape[1]], F32, name=name)
             nc.vector.scalar_tensor_tensor(
                 out=weighted[:],
                 in0=acc,
                 scalar=1.0,
-                in1=volt_sb[:, first : first + width],
+                in1=weight,
                 op0=MULT,
                 op1=MULT,
-                accum_out=parts[:, part : part + 1],
+                accum_out=total,
             )
 
-        def balance_on_vector(part):
+        def balance_on_vector(total):
             difference = small.tile([P, HALF], F32)
             nc.vector.scalar_tensor_tensor(
                 out=difference[:],
-                in0=gens_sb[:, 0:HALF],
+                in0=gens_sb[:, HALF:K],
                 scalar=-1.0,
-                in1=loads_sb[:, 0:HALF],
+                in1=loads_sb[:, HALF:K],
                 op0=MULT,
                 op1=ADD,
-                accum_out=parts[:, part : part + 1],
+                accum_out=total,
             )
 
-        def balance_on_scalar(part):
+        def balance_on_scalar(totals):
             for n, (source, sign) in enumerate(((loads_sb, 1.0), (gens_sb, -1.0))):
                 signed = small.tile([P, HALF], F32, name="signed%d" % n)
                 nc.scalar.activation(
                     out=signed[:],
-                    in_=source[:, HALF:K],
+                    in_=source[:, 0:HALF],
                     func=mybir.ActivationFunctionType.Copy,
                     scale=sign,
-                    accum_out=parts[:, part + n : part + n + 1],
+                    accum_out=totals[:, n : n + 1],
                 )
 
-        for j in range(BLOCKS - 1):
-            flip(j)
-            quantise(j)
-        flip(BLOCKS - 1)
-        balance_on_vector(2)
-        quantise(BLOCKS - 1)
-        balance_on_scalar(8)
+        waiting = None
+        for j in range(LAST):
+            flipped = flip(rows_sb[j][0])
+            on_vector = j in ON_VECTOR
+            if waiting is not None and not on_vector:
+                quantise(*waiting)
+                waiting = None
+            grouped = copy_out(flipped, PASSES, nc.vector.tensor_copy if on_vector else nc.scalar.copy)
+            if waiting is not None:
+                quantise(*waiting)
+            waiting = (j, 0, PASSES, grouped)
+        quantise(*waiting)
+        flipped_a = flip(rows_sb[LAST][0])
+        flipped_b = flip(rows_sb[LAST][1])
+        grouped_a = copy_out(flipped_a, 1, nc.scalar.copy)
+        grouped_b = copy_out(flipped_b, 1, nc.vector.tensor_copy)
+        quantise(LAST, 0, 1, grouped_a)
+        quantise(LAST, 1, 1, grouped_b)
+        balance_on_scalar(parts[:, 0:2])
+        balance_on_vector(parts[:, 2:3])
 
         acc_early = acc_psum.tile([P, EARLY * P], F32)
         for t in range(EARLY):
             multiply(t, acc_early[:, t * P : (t + 1) * P])
-        acc_last = acc_psum.tile([P, P], F32)
-        multiply(EARLY, acc_last[:])
-        weigh(acc_early[:], 0, EARLY * P, 0)
-        weigh(acc_last[:], EARLY * P, P, 1)
+        multiply(EARLY, acc_last[:, 0:P])
+        weigh(acc_early[:], volt_sb[:, 0 : EARLY * P], parts[:, 3:4], "weighted_early")
+        weigh(acc_last[:], weights[:], column[:, 0:1], "weighted_last")
 
-        nc.vector.tensor_reduce(out=column[:, 0:1], in_=parts[:], axis=mybir.AxisListType.X, op=ADD)
         turned = small.tile([P, QUAD], F32, align_bytes=64)
         nc.vector.transpose(out=turned[:], in_=column[:])
         nc.sync.dma_start(out=out.rearrange("(q r) -> q r", r=QUAD), in_=turned[0:P:QUAD, :])

@@ -23,6 +23,7 @@ EARLY = ROUNDS - 1
 HALF = K // 2
 PARTS = 4
 ON_VECTOR = (3,)
+WARM_UP = 4
 QUAD = 32
 
 FLOPS = 2 * 2 * P * NB * K
@@ -44,6 +45,12 @@ def tile_kktloss_pc_s_kernel(tc, Volt, Y_top, Yconj_top, PQ_Loads, PQ_Gens, out)
         make_identity(nc, ident[:])
         ones = consts.tile([P, PARTS], F32)
         nc.gpsimd.memset(ones[:], 1.0)
+
+        zeros = consts.tile([P, P], F32)
+        nc.vector.memset(zeros[:], 0.0)
+        warm = flip_psum.tile([P, 2 * PASSES, P], F32, name="flipped")
+        for n in range(WARM_UP):
+            nc.tensor.matmul(warm[:, n % 4, :], lhsT=zeros[:], rhs=zeros[:], start=True, stop=True)
 
         sources = [Volt[:, :]]
         for t in range(ROUNDS):

@@ -48,9 +48,14 @@ def tile_kktloss_pc_s_kernel(tc, Volt, Y_top, Yconj_top, PQ_Loads, PQ_Gens, out)
 
         zeros = consts.tile([P, P], F32)
         nc.vector.memset(zeros[:], 0.0)
-        warm = flip_psum.tile([P, 2 * PASSES, P], F32, name="flipped")
+        acc_last = acc_psum.tile([P, K_PASS], F32)
+
+        def keep_warm(width):
+            idle = acc_last[:, 2 * P : 2 * P + width]
+            nc.tensor.matmul(idle, lhsT=zeros[:], rhs=zeros[:, 0:width], start=True, stop=True)
+
         for n in range(WARM_UP):
-            nc.tensor.matmul(warm[:, n % 4, :], lhsT=zeros[:], rhs=zeros[:], start=True, stop=True)
+            keep_warm(P)
 
         sources = [Volt[:, :]]
         for t in range(ROUNDS):
@@ -77,8 +82,8 @@ def tile_kktloss_pc_s_kernel(tc, Volt, Y_top, Yconj_top, PQ_Loads, PQ_Gens, out)
         column = small.tile([P, QUAD], F32, align_bytes=64)
         nc.vector.memset(column[:], 0.0)
 
-        acc_last = acc_psum.tile([P, P + PARTS], F32)
-        nc.tensor.matmul(acc_last[:, P:], lhsT=ident[:], rhs=ones[:], start=True, stop=True)
+        products = acc_last[:, 0 : P + PARTS]
+        nc.tensor.matmul(products[:, P:], lhsT=ident[:], rhs=ones[:], start=True, stop=True)
         weights = small.tile([P, P + PARTS], F32)
         nc.gpsimd.tensor_copy(out=weights[:, 0:P], in_=volt_sb[:, EARLY * P : NB])
         parts = weights[:, P : P + PARTS]
@@ -162,6 +167,8 @@ def tile_kktloss_pc_s_kernel(tc, Volt, Y_top, Yconj_top, PQ_Loads, PQ_Gens, out)
         waiting = None
         for j in range(LAST):
             flipped = flip(rows_sb[j][0])
+            if j % 2 == 0:
+                keep_warm(P // 2)
             on_vector = j in ON_VECTOR
             if waiting is not None and not on_vector:
                 quantise(*waiting)
@@ -185,7 +192,7 @@ def tile_kktloss_pc_s_kernel(tc, Volt, Y_top, Yconj_top, PQ_Loads, PQ_Gens, out)
             multiply(t, acc_early[:, t * P : (t + 1) * P])
         multiply(EARLY, acc_last[:, 0:P])
         weigh(acc_early[:], volt_sb[:, 0 : EARLY * P], parts[:, 3:4], "weighted_early")
-        weigh(acc_last[:], weights[:], column[:, 0:1], "weighted_last")
+        weigh(products, weights[:], column[:, 0:1], "weighted_last")
 
         turned = small.tile([P, QUAD], F32, align_bytes=64)
         nc.vector.transpose(out=turned[:], in_=column[:])

@@ -19,11 +19,14 @@ PASSES = K // K_PASS
 ROUNDS = NB // P
 BLOCKS = 1 + 2 * ROUNDS
 LAST = BLOCKS - 1
-EARLY = ROUNDS - 1
-HALF = K // 2
-PARTS = 4
+PAIR = 2
+PAIR_ROWS = PAIR * P
+EARLY_COLUMNS = 384
+SPLIT = 832
+PARTS = 5
 ON_VECTOR = (3,)
 WARM_UP = 4
+HOLD = (2, 4, 6,)
 QUAD = 32
 
 FLOPS = 2 * 2 * P * NB * K
@@ -51,7 +54,7 @@ def tile_kktloss_pc_s_kernel(tc, Volt, Y_top, Yconj_top, PQ_Loads, PQ_Gens, out)
         acc_last = acc_psum.tile([P, K_PASS], F32)
 
         def keep_warm(width):
-            idle = acc_last[:, 2 * P : 2 * P + width]
+            idle = acc_last[:, 3 * P : 3 * P + width]
             nc.tensor.matmul(idle, lhsT=zeros[:], rhs=zeros[:, 0:width], start=True, stop=True)
 
         for n in range(WARM_UP):
@@ -61,32 +64,36 @@ def tile_kktloss_pc_s_kernel(tc, Volt, Y_top, Yconj_top, PQ_Loads, PQ_Gens, out)
         for t in range(ROUNDS):
             sources.append(Y_top[t * P : (t + 1) * P, :])
             sources.append(Yconj_top[t * P : (t + 1) * P, :])
+        loads_sb = loads.tile([P, K], BF16)
+        gens_sb = loads.tile([P, K], BF16)
         rows_sb = []
         for j in range(BLOCKS):
             pieces = PASSES if j == LAST else 1
             width = K // pieces
             tiles = []
+            if j == LAST:
+                nc.sync.dma_start(out=loads_sb[:, 0:EARLY_COLUMNS], in_=PQ_Loads[:, 0:EARLY_COLUMNS])
+                nc.sync.dma_start(out=gens_sb[:, 0:EARLY_COLUMNS], in_=PQ_Gens[:, 0:EARLY_COLUMNS])
             for n in range(pieces):
                 piece = loads.tile([P, width], BF16, name="rows%d_%d" % (j, n))
                 nc.sync.dma_start(out=piece[:], in_=sources[j][:, n * width : (n + 1) * width])
                 tiles.append(piece)
             rows_sb.append(tiles)
         volt_sb = rows_sb[0][0]
-        loads_sb = loads.tile([P, K], BF16)
-        gens_sb = loads.tile([P, K], BF16)
-        nc.sync.dma_start(out=loads_sb[:], in_=PQ_Loads[:, :])
-        nc.sync.dma_start(out=gens_sb[:], in_=PQ_Gens[:, :])
+        nc.sync.dma_start(out=loads_sb[:, EARLY_COLUMNS:K], in_=PQ_Loads[:, EARLY_COLUMNS:K])
+        nc.sync.dma_start(out=gens_sb[:, EARLY_COLUMNS:K], in_=PQ_Gens[:, EARLY_COLUMNS:K])
 
         codes = keep.tile([P, BLOCKS, PASSES * P], U32, align_bytes=64)
         scales = keep.tile([P, BLOCKS, PASSES * P], U8, align_bytes=64)
         column = small.tile([P, QUAD], F32, align_bytes=64)
         nc.vector.memset(column[:], 0.0)
 
-        products = acc_last[:, 0 : P + PARTS]
-        nc.tensor.matmul(products[:, P:], lhsT=ident[:], rhs=ones[:], start=True, stop=True)
-        weights = small.tile([P, P + PARTS], F32)
-        nc.gpsimd.tensor_copy(out=weights[:, 0:P], in_=volt_sb[:, EARLY * P : NB])
-        parts = weights[:, P : P + PARTS]
+        acc_first = acc_psum.tile([P, PAIR_ROWS], F32)
+        products = acc_last[:, 0 : PAIR_ROWS + PARTS]
+        nc.tensor.matmul(products[:, PAIR_ROWS:], lhsT=ident[:], rhs=ones[:], start=True, stop=True)
+        weights = small.tile([P, PAIR_ROWS + PARTS], F32)
+        nc.scalar.copy(out=weights[:, 0:PAIR_ROWS], in_=volt_sb[:, PAIR_ROWS:NB])
+        parts = weights[:, PAIR_ROWS:]
 
         def flip(piece):
             words = piece[:].bitcast(F32)
@@ -114,7 +121,8 @@ def tile_kktloss_pc_s_kernel(tc, Volt, Y_top, Yconj_top, PQ_Loads, PQ_Gens, out)
                 in_=grouped[:, 0 : passes * K_PASS],
             )
 
-        def multiply(t, acc):
+        def multiply(t):
+            acc = (acc_first if t < PAIR else acc_last)[:, (t % PAIR) * P : (t % PAIR + 1) * P]
             for which in range(2):
                 j = 1 + 2 * t + which
                 for g in range(PASSES):
@@ -141,24 +149,24 @@ def tile_kktloss_pc_s_kernel(tc, Volt, Y_top, Yconj_top, PQ_Loads, PQ_Gens, out)
                 accum_out=total,
             )
 
-        def balance_on_vector(total):
-            difference = small.tile([P, HALF], F32)
+        def balance_on_vector(first, end, total):
+            difference = small.tile([P, end - first], F32, name="difference%d" % first)
             nc.vector.scalar_tensor_tensor(
                 out=difference[:],
-                in0=gens_sb[:, HALF:K],
+                in0=gens_sb[:, first:end],
                 scalar=-1.0,
-                in1=loads_sb[:, HALF:K],
+                in1=loads_sb[:, first:end],
                 op0=MULT,
                 op1=ADD,
                 accum_out=total,
             )
 
-        def balance_on_scalar(totals):
+        def balance_on_scalar(first, end, totals):
             for n, (source, sign) in enumerate(((loads_sb, 1.0), (gens_sb, -1.0))):
-                signed = small.tile([P, HALF], F32, name="signed%d" % n)
+                signed = small.tile([P, end - first], F32, name="signed%d" % n)
                 nc.scalar.activation(
                     out=signed[:],
-                    in_=source[:, 0:HALF],
+                    in_=source[:, first:end],
                     func=mybir.ActivationFunctionType.Copy,
                     scale=sign,
                     accum_out=totals[:, n : n + 1],
@@ -167,31 +175,26 @@ def tile_kktloss_pc_s_kernel(tc, Volt, Y_top, Yconj_top, PQ_Loads, PQ_Gens, out)
         waiting = None
         for j in range(LAST):
             flipped = flip(rows_sb[j][0])
-            if j % 2 == 0:
-                keep_warm(P // 2)
             on_vector = j in ON_VECTOR
-            if waiting is not None and not on_vector:
-                quantise(*waiting)
-                waiting = None
-            grouped = copy_out(flipped, PASSES, nc.vector.tensor_copy if on_vector else nc.scalar.copy)
+            if on_vector:
+                grouped = copy_out(flipped, PASSES, nc.vector.tensor_copy)
             if waiting is not None:
                 quantise(*waiting)
+            if not on_vector:
+                grouped = copy_out(flipped, PASSES, nc.scalar.copy)
             waiting = (j, 0, PASSES, grouped)
+            if j in HOLD:
+                keep_warm(P // 2)
+        balance_on_vector(0, EARLY_COLUMNS, parts[:, 4:5])
         quantise(*waiting)
-        flipped_a = flip(rows_sb[LAST][0])
-        flipped_b = flip(rows_sb[LAST][1])
-        grouped_a = copy_out(flipped_a, 1, nc.scalar.copy)
-        grouped_b = copy_out(flipped_b, 1, nc.vector.tensor_copy)
-        quantise(LAST, 0, 1, grouped_a)
-        quantise(LAST, 1, 1, grouped_b)
-        balance_on_scalar(parts[:, 0:2])
-        balance_on_vector(parts[:, 2:3])
-
-        acc_early = acc_psum.tile([P, EARLY * P], F32)
-        for t in range(EARLY):
-            multiply(t, acc_early[:, t * P : (t + 1) * P])
-        multiply(EARLY, acc_last[:, 0:P])
-        weigh(acc_early[:], volt_sb[:, 0 : EARLY * P], parts[:, 3:4], "weighted_early")
+        halves = [copy_out(flip(piece), 1, nc.scalar.copy) for piece in rows_sb[LAST]]
+        for g in range(PASSES):
+            quantise(LAST, g, 1, halves[g])
+        balance_on_scalar(EARLY_COLUMNS, SPLIT, parts[:, 0:2])
+        balance_on_vector(SPLIT, K, parts[:, 2:3])
+        for t in range(ROUNDS):
+            multiply(t)
+        weigh(acc_first[:], volt_sb[:, 0:PAIR_ROWS], parts[:, 3:4], "weighted_first")
         weigh(products, weights[:], column[:, 0:1], "weighted_last")
 
         turned = small.tile([P, QUAD], F32, align_bytes=64)

from contextlib import ExitStack

import concourse.mybir as mybir
from concourse.masks import make_identity

F32 = mybir.dt.float32
BF16 = mybir.dt.bfloat16
U32 = mybir.dt.uint32
U8 = mybir.dt.uint8
FP8X4 = mybir.dt.float8_e4m3fn_x4
MULT = mybir.AluOpType.mult
ADD = mybir.AluOpType.add

P = 128
K = 1024
NB = 512
K_PASS = 512
PASSES = K // K_PASS
ROUNDS = NB // P
BLOCKS = 1 + 2 * ROUNDS
LAST = BLOCKS - 1
PAIR = 2
PAIR_ROWS = PAIR * P
EARLY_COLUMNS = 384
SPLIT = 832
PARTS = 5
ON_VECTOR = (3,)
WARM_UP = 4
HOLD = (2, 4, 6,)
QUAD = 32

FLOPS = 2 * 2 * P * NB * K


def tile_kktloss_pc_s_kernel(tc, Volt, Y_top, Yconj_top, PQ_Loads, PQ_Gens, out):
    nc = tc.nc
    with ExitStack() as ctx:
        consts = ctx.enter_context(tc.tile_pool(name="consts", bufs=1))
        loads = ctx.enter_context(tc.tile_pool(name="loads", bufs=1))
        stage = ctx.enter_context(tc.tile_pool(name="stage", bufs=4))
        keep = ctx.enter_context(tc.tile_pool(name="keep", bufs=1))
        small = ctx.enter_context(tc.tile_pool(name="small", bufs=1))
        flip_psum = ctx.enter_context(tc.psum_pool(name="flip_psum", bufs=6))
        acc_psum = ctx.enter_context(tc.psum_pool(name="acc_psum", bufs=1))
        ctx.enter_context(tc.manual_schedule())

        ident = consts.tile([P, P], F32)
        make_identity(nc, ident[:])
        ones = consts.tile([P, PARTS], F32)
        nc.gpsimd.memset(ones[:], 1.0)

        zeros = consts.tile([P, P], F32)
        nc.vector.memset(zeros[:], 0.0)
        acc_last = acc_psum.tile([P, K_PASS], F32)

        def keep_warm(width):
            idle = acc_last[:, 3 * P : 3 * P + width]
            nc.tensor.matmul(idle, lhsT=zeros[:], rhs=zeros[:, 0:width], start=True, stop=True)

        for n in range(WARM_UP):
            keep_warm(P)

        sources = [Volt[:, :]]
        for t in range(ROUNDS):
            sources.append(Y_top[t * P : (t + 1) * P, :])
            sources.append(Yconj_top[t * P : (t + 1) * P, :])
        loads_sb = loads.tile([P, K], BF16)
        gens_sb = loads.tile([P, K], BF16)
        rows_sb = []
        for j in range(BLOCKS):
            pieces = PASSES if j == LAST else 1
            width = K // pieces
            tiles = []
            if j == LAST:
                nc.sync.dma_start(out=loads_sb[:, 0:EARLY_COLUMNS], in_=PQ_Loads[:, 0:EARLY_COLUMNS])
                nc.sync.dma_start(out=gens_sb[:, 0:EARLY_COLUMNS], in_=PQ_Gens[:, 0:EARLY_COLUMNS])
            for n in range(pieces):
                piece = loads.tile([P, width], BF16, name="rows%d_%d" % (j, n))
                nc.sync.dma_start(out=piece[:], in_=sources[j][:, n * width : (n + 1) * width])
                tiles.append(piece)
            rows_sb.append(tiles)
        volt_sb = rows_sb[0][0]
        nc.sync.dma_start(out=loads_sb[:, EARLY_COLUMNS:K], in_=PQ_Loads[:, EARLY_COLUMNS:K])
        nc.sync.dma_start(out=gens_sb[:, EARLY_COLUMNS:K], in_=PQ_Gens[:, EARLY_COLUMNS:K])

        codes = keep.tile([P, BLOCKS, PASSES * P], U32, align_bytes=64)
        scales = keep.tile([P, BLOCKS, PASSES * P], U8, align_bytes=64)
        column = small.tile([P, QUAD], F32, align_bytes=64)
        nc.vector.memset(column[:], 0.0)

        acc_first = acc_psum.tile([P, PAIR_ROWS], F32)
        products = acc_last[:, 0 : PAIR_ROWS + PARTS]
        nc.tensor.matmul(products[:, PAIR_ROWS:], lhsT=ident[:], rhs=ones[:], start=True, stop=True)
        weights = small.tile([P, PAIR_ROWS + PARTS], F32)
        nc.scalar.copy(out=weights[:, 0:PAIR_ROWS], in_=volt_sb[:, PAIR_ROWS:NB])
        parts = weights[:, PAIR_ROWS:]

        def flip(piece):
            words = piece[:].bitcast(F32)
            flipped = flip_psum.tile([P, 2 * PASSES, P], F32, name="flipped")
            for g in range(piece.shape[1] // K_PASS):
                for u in range(2):
                    every_2nd = words[:, 2 * P * g + u : 2 * P * (g + 1) : 2]
                    nc.tensor.transpose(flipped[:, 2 * g + u, :], every_2nd, ident[:])
            return flipped

        def copy_out(flipped, passes, copy):
            grouped = stage.tile([P, K], BF16, align_bytes=64, name="grouped")
            words = grouped[:].bitcast(F32).rearrange("p (g r u) -> p g r u", g=PASSES, u=2)
            copy(
                out=words[:, 0:passes],
                in_=flipped[:, 0 : 2 * passes].rearrange("p (g u) r -> p g r u", u=2),
            )
            return grouped

        def quantise(j, first, passes, grouped):
            cols = slice(first * P, (first + passes) * P)
            nc.vector.quantize_mx(
                out=codes[:, j, cols].bitcast(FP8X4),
                scales=scales[:, j, cols],
                in_=grouped[:, 0 : passes * K_PASS],
            )

        def multiply(t):
            acc = (acc_first if t < PAIR else acc_last)[:, (t % PAIR) * P : (t % PAIR + 1) * P]
            for which in range(2):
                j = 1 + 2 * t + which
                for g in range(PASSES):
                    cols = slice(g * P, (g + 1) * P)
                    nc.tensor.matmul_mx(
                        out=acc,
                        lhsT=codes[:, 0, cols].bitcast(FP8X4),
                        lhsT_scale=scales[:, 0, cols],
                        rhs=codes[:, j, cols].bitcast(FP8X4),
                        rhs_scale=scales[:, j, cols],
                        start=(which == 0 and g == 0),
                        stop=(which == 1 and g == PASSES - 1),
                    )

        def weigh(acc, weight, total, name):
            weighted = small.tile([P, acc.shape[1]], F32, name=name)
            nc.vector.scalar_tensor_tensor(
                out=weighted[:],
                in0=acc,
                scalar=1.0,
                in1=weight,
                op0=MULT,
                op1=MULT,
                accum_out=total,
            )

        def balance_on_vector(first, end, total):
            difference = small.tile([P, end - first], F32, name="difference%d" % first)
            nc.vector.scalar_tensor_tensor(
                out=difference[:],
                in0=gens_sb[:, first:end],
                scalar=-1.0,
                in1=loads_sb[:, first:end],
                op0=MULT,
                op1=ADD,
                accum_out=total,
            )

        def balance_on_scalar(first, end, totals):
            for n, (source, sign) in enumerate(((loads_sb, 1.0), (gens_sb, -1.0))):
                signed = small.tile([P, end - first], F32, name="signed%d" % n)
                nc.scalar.activation(
                    out=signed[:],
                    in_=source[:, first:end],
                    func=mybir.ActivationFunctionType.Copy,
                    scale=sign,
                    accum_out=totals[:, n : n + 1],
                )

        waiting = None
        for j in range(LAST):
            flipped = flip(rows_sb[j][0])
            on_vector = j in ON_VECTOR
            if on_vector:
                grouped = copy_out(flipped, PASSES, nc.vector.tensor_copy)
            if waiting is not None:
                quantise(*waiting)
            if not on_vector:
                grouped = copy_out(flipped, PASSES, nc.scalar.copy)
            waiting = (j, 0, PASSES, grouped)
            if j in HOLD:
                keep_warm(P // 2)
        balance_on_vector(0, EARLY_COLUMNS, parts[:, 4:5])
        quantise(*waiting)
        halves = [copy_out(flip(piece), 1, nc.scalar.copy) for piece in rows_sb[LAST]]
        for g in range(PASSES):
            quantise(LAST, g, 1, halves[g])
        balance_on_scalar(EARLY_COLUMNS, SPLIT, parts[:, 0:2])
        balance_on_vector(SPLIT, K, parts[:, 2:3])
        for t in range(ROUNDS):
            multiply(t)
        weigh(acc_first[:], volt_sb[:, 0:PAIR_ROWS], parts[:, 3:4], "weighted_first")
        weigh(products, weights[:], column[:, 0:1], "weighted_last")

        turned = small.tile([P, QUAD], F32, align_bytes=64)
        nc.vector.transpose(out=turned[:], in_=column[:])
        nc.sync.dma_start(out=out.rearrange("(q r) -> q r", r=QUAD), in_=turned[0:P:QUAD, :])
